import numpy as np
import ml_dtypes


def mxq(x, axis, fmt="e4m3"):
    dtype, down = {"e4m3": (ml_dtypes.float8_e4m3fn, 7), "e5m2": (ml_dtypes.float8_e5m2, 14)}[fmt]
    v = np.moveaxis(np.asarray(x, np.float32).astype(ml_dtypes.bfloat16).astype(np.float64), axis, -1)
    blocks = v.reshape(v.shape[:-1] + (-1, 32))
    amax = np.abs(blocks).max(-1, keepdims=True)
    byte = np.maximum(np.where(amax > 0, np.frexp(amax)[1] - 1 + 127, 0) - down, 1)
    scale = np.exp2(byte - 127.0)
    codes = (blocks / scale).astype(np.float32).astype(dtype).astype(np.float64)
    return np.moveaxis((codes * scale).reshape(v.shape), -1, axis)


WIDE = False


def mx_kscale(k):
    if not WIDE:
        return np.ones(k)
    levels = np.array([10, -10, 5, -5, 0])
    if k % 512:
        return np.exp2(np.random.permutation(np.resize(levels, k // 32))).repeat(32)
    a = np.empty((k // 512, 16))
    for p in range(k // 512):
        a[p, :8] = np.random.permutation(np.resize(levels, 8))
        for g in range(8):
            far = levels[np.abs(levels - a[p, g]) >= 10]
            a[p, g + 8] = far[np.random.randint(len(far))]
    return np.exp2(a.ravel()).repeat(32)


BF16 = ml_dtypes.bfloat16


def bf(x):
    return np.asarray(x, np.float32).astype(BF16)


def f64(x):
    return np.asarray(x).astype(np.float64)


BS, DC, R, C = 1, 128, 64, 64
N = R * C
THRESH = 0.85


def setup_inputs():
    s = mx_kscale(N)
    u = s / s.min()
    g = 2.0 ** np.round(np.log2(u.mean()))
    seg = np.random.standard_normal((BS, DC, R, C)) * 0.1 * np.sqrt(N)
    W0 = f64(bf(np.random.random_sample((BS, N, N))))
    return {"seg": bf(seg * (g / u).reshape(1, 1, R, C)),
            "W": bf(np.where(W0 > THRESH, W0 * u, W0))}


def reference(seg, W):
    seg, W = f64(seg), f64(W)
    bs, d, r, c = seg.shape
    Wt = np.where(W > THRESH, W, 0.0)
    D = Wt / Wt.sum(axis=-1, keepdims=True)
    seg_flat = seg.reshape(bs, d, r * c)
    out = mxq(seg_flat, 2, "e4m3") @ mxq(D, 2, "e4m3").transpose(0, 2, 1)
    return out.reshape(bs, d, r, c)

@@ -1,0 +1,203 @@
+from contextlib import ExitStack
+
+import concourse.mybir as mybir
+from concourse.masks import make_identity
+
+BF16 = mybir.dt.bfloat16
+F32 = mybir.dt.float32
+U32 = mybir.dt.uint32
+U8 = mybir.dt.uint8
+FP8X4 = mybir.dt.float8_e4m3fn_x4
+ALU = mybir.AluOpType
+ACT = mybir.ActivationFunctionType
+
+P = 128
+N = 4096
+HALF = N // 2
+WORDS = N // 2
+THRESH = 0.85
+TILES = N // P
+LAST = TILES - 1
+PASSES = N // 512
+BANKS = 4
+FLOPS = 2 * P * N * N
+
+AHEAD = 4
+V_COLS = 768
+CUT = N - V_COLS
+
+
+def tile_regu_diff_kernel(tc, seg, W, out):
+    nc = tc.nc
+    seg_flat = seg.rearrange("b d r c -> (b d) (r c)")
+    out_flat = out.rearrange("b d r c -> (b d) (r c)")
+    w2 = W.rearrange("b m n -> (b m) n")
+
+    with ExitStack() as ctx:
+        ctx.enter_context(tc.manual_schedule())
+        const = ctx.enter_context(tc.tile_pool(name="const", bufs=1))
+        win_pool = ctx.enter_context(tc.tile_pool(name="win", bufs=AHEAD + 2))
+        wt_pool = ctx.enter_context(tc.tile_pool(name="wt", bufs=3))
+        d_pool = ctx.enter_context(tc.tile_pool(name="d", bufs=3))
+        g_pool = ctx.enter_context(tc.tile_pool(name="grouped", bufs=4))
+        q_pool = ctx.enter_context(tc.tile_pool(name="quant", bufs=3))
+        res_pool = ctx.enter_context(tc.tile_pool(name="res", bufs=2))
+        psum_t = ctx.enter_context(tc.psum_pool(name="psum_t", bufs=6))
+        psum_a = ctx.enter_context(tc.psum_pool(name="psum_a", bufs=2))
+
+        ident = const.tile([P, P], F32, name="ident")
+        make_identity(nc, ident[:])
+        part = const.tile([P, TILES], F32, name="part")
+        halves = const.tile([P, 2], F32, name="halves")
+        recip = const.tile([P, TILES], F32, name="recip")
+        seg_in = const.tile([P, N], BF16, name="seg_in")
+        seg_codes = const.tile([P, PASSES * P], U32, name="seg_codes", align_bytes=64)
+        seg_scales = const.tile([P, PASSES * P], U8, name="seg_scales", align_bytes=64)
+
+        wins = {}
+        wts = {}
+        ds = {}
+        groupeds = {}
+        banks_of = {}
+        quants = {}
+        accs = {}
+
+        def load(t):
+            wins[t] = win_pool.tile([P, N], BF16, name="win")
+            pieces = 2 if t == 0 else 1
+            width = N // pieces
+            for i in range(pieces):
+                cols = slice(i * width, (i + 1) * width)
+                nc.sync.dma_start(out=wins[t][:, cols], in_=w2[t * P : (t + 1) * P, cols])
+
+        def threshold_cols(t, cols, total):
+            nc.vector.scalar_tensor_tensor(
+                out=wts[t][:, cols],
+                in0=wins[t][:, cols],
+                scalar=THRESH,
+                in1=wins[t][:, cols],
+                op0=ALU.is_gt,
+                op1=ALU.mult,
+                accum_out=total,
+            )
+
+        def threshold(t):
+            wts[t] = wt_pool.tile([P, N], BF16, name="wt")
+            if t == 0:
+                for i in range(2):
+                    threshold_cols(t, slice(i * HALF, (i + 1) * HALF), halves[:, i : i + 1])
+                nc.vector.tensor_tensor(
+                    out=part[:, 0:1], in0=halves[:, 0:1], in1=halves[:, 1:2], op=ALU.add
+                )
+            else:
+                threshold_cols(t, slice(0, N), part[:, t : t + 1])
+
+        def reciprocal(t):
+            nc.vector.reciprocal(out=recip[:, t : t + 1], in_=part[:, t : t + 1])
+
+        def scale_scalar(t):
+            ds[t] = d_pool.tile([P, N], BF16, name="d")
+            if t != LAST:
+                nc.scalar.activation(
+                    out=ds[t][:, :CUT], in_=wts[t][:, :CUT], func=ACT.Copy, scale=recip[:, t : t + 1]
+                )
+
+        def scale_vector(t):
+            pieces = [slice(CUT, N)]
+            if t == LAST:
+                pieces = [slice(i * 1024, (i + 1) * 1024) for i in range(BANKS)]
+            for cols in pieces:
+                nc.vector.tensor_scalar(
+                    out=ds[t][:, cols], in0=wts[t][:, cols], scalar1=recip[:, t : t + 1], scalar2=None, op0=ALU.mult
+                )
+
+        def turn(key, rows):
+            words = rows[:].bitcast(F32)
+            banks_of[key] = []
+            for bank in range(BANKS):
+                xt = psum_t.tile([P, 2, 2, P], F32, name="xt")
+                for gl in range(2):
+                    w0 = 256 * (2 * bank + gl)
+                    for u in range(2):
+                        nc.tensor.transpose(xt[:, gl, u, :], words[:, w0 + u : w0 + 256 : 2], ident[:])
+                banks_of[key].append(xt)
+
+        def evacuate(key):
+            groupeds[key] = g_pool.tile([P, PASSES * 512], BF16, name="grouped", align_bytes=64)
+            view = groupeds[key][:].bitcast(F32).rearrange("p (b g r u) -> p b g r u", b=BANKS, g=2, u=2)
+            for bank in range(BANKS):
+                nc.scalar.copy(
+                    out=view[:, bank, :, :, :], in_=banks_of[key][bank][:].rearrange("p g u r -> p g r u")
+                )
+
+        def quantise(t):
+            codes = q_pool.tile([P, PASSES * P], U32, name="codes", align_bytes=64)
+            scales = q_pool.tile([P, PASSES * P], U8, name="scales", align_bytes=64)
+            pieces = 4 if t == LAST else 1
+            words = PASSES * P // pieces
+            for i in range(pieces):
+                nc.vector.quantize_mx(
+                    out=codes[:, i * words : (i + 1) * words].bitcast(FP8X4),
+                    scales=scales[:, i * words : (i + 1) * words],
+                    in_=groupeds[t][:, 4 * i * words : 4 * (i + 1) * words],
+                )
+            quants[t] = (codes, scales)
+
+        def multiply(t):
+            if t % 4 == 0:
+                accs[t // 4] = psum_a.tile([P, 512], F32, name="acc")
+            acc = accs[t // 4]
+            codes, scales = quants[t]
+            c0 = (t % 4) * P
+            for g in range(PASSES):
+                cols = slice(g * P, (g + 1) * P)
+                nc.tensor.matmul_mx(
+                    out=acc[:, c0 : c0 + P],
+                    lhsT=seg_codes[:, cols].bitcast(FP8X4),
+                    lhsT_scale=seg_scales[:, cols],
+                    rhs=codes[:, cols].bitcast(FP8X4),
+                    rhs_scale=scales[:, cols],
+                    start=(g == 0),
+                    stop=(g == PASSES - 1),
+                )
+
+        def store(q, c0, c1):
+            res = res_pool.tile([P, 512], F32, name="res")
+            nc.scalar.copy(out=res[:, c0:c1], in_=accs[q][:, c0:c1])
+            nc.sync.dma_start(out=out_flat[:, 512 * q + c0 : 512 * q + c1], in_=res[:, c0:c1])
+
+        load(0)
+        nc.sync.dma_start(out=seg_in[:], in_=seg_flat)
+        for t in range(1, AHEAD):
+            load(t)
+        turn("seg", seg_in)
+        evacuate("seg")
+
+        for s in range(TILES + 3):
+            if s + AHEAD < TILES:
+                load(s + AHEAD)
+            if s < TILES:
+                threshold(s)
+            if s == 1:
+                nc.vector.quantize_mx(
+                    out=seg_codes[:].bitcast(FP8X4), scales=seg_scales[:], in_=groupeds["seg"][:]
+                )
+            if 0 <= s - 3:
+                quantise(s - 3)
+            if s < TILES:
+                reciprocal(s)
+                scale_scalar(s)
+            if 0 <= s - 1 < TILES:
+                scale_vector(s - 1)
+                turn(s - 1, ds[s - 1])
+            if 0 <= s - 3:
+                multiply(s - 3)
+            if 0 <= s - 1 < TILES:
+                evacuate(s - 1)
+            done = s - 3
+            if 0 <= done < TILES - 4 and done % 4 == 3:
+                store(done // 4, 0, 512)
+            if done == TILES - 2:
+                store(done // 4, 0, 384)
+            if done == TILES - 1:
+                store(done // 4, 384, 512)

@@ -18,13 +18,13 @@ WORDS = N // 2
 THRESH = 0.85
 TILES = N // P
 LAST = TILES - 1
+FOLDED = (0, LAST - 1, LAST)
 PASSES = N // 512
 BANKS = 4
 FLOPS = 2 * P * N * N
 
 AHEAD = 4
-V_COLS = 768
-CUT = N - V_COLS
+V_COLS = 1664
 
 
 def tile_regu_diff_kernel(tc, seg, W, out):
@@ -37,16 +37,19 @@ def tile_regu_diff_kernel(tc, seg, W, out):
         ctx.enter_context(tc.manual_schedule())
         const = ctx.enter_context(tc.tile_pool(name="const", bufs=1))
         win_pool = ctx.enter_context(tc.tile_pool(name="win", bufs=AHEAD + 2))
-        wt_pool = ctx.enter_context(tc.tile_pool(name="wt", bufs=3))
-        d_pool = ctx.enter_context(tc.tile_pool(name="d", bufs=3))
+        wt_pool = ctx.enter_context(tc.tile_pool(name="wt", bufs=4))
+        d_pool = ctx.enter_context(tc.tile_pool(name="d", bufs=4))
         g_pool = ctx.enter_context(tc.tile_pool(name="grouped", bufs=4))
-        q_pool = ctx.enter_context(tc.tile_pool(name="quant", bufs=3))
+        q_pool = ctx.enter_context(tc.tile_pool(name="quant", bufs=4))
+        mask_pool = ctx.enter_context(tc.tile_pool(name="mask", bufs=2))
         res_pool = ctx.enter_context(tc.tile_pool(name="res", bufs=2))
         psum_t = ctx.enter_context(tc.psum_pool(name="psum_t", bufs=6))
         psum_a = ctx.enter_context(tc.psum_pool(name="psum_a", bufs=2))
 
         ident = const.tile([P, P], F32, name="ident")
         make_identity(nc, ident[:])
+        ident_bf = const.tile([P, P], BF16, name="ident_bf")
+        make_identity(nc, ident_bf[:])
         part = const.tile([P, TILES], F32, name="part")
         halves = const.tile([P, 2], F32, name="halves")
         recip = const.tile([P, TILES], F32, name="recip")
@@ -64,7 +67,7 @@ def tile_regu_diff_kernel(tc, seg, W, out):
 
         def load(t):
             wins[t] = win_pool.tile([P, N], BF16, name="win")
-            pieces = 2 if t == 0 else 1
+            pieces = {0: 4, 1: 2}.get(t, 1)
             width = N // pieces
             for i in range(pieces):
                 cols = slice(i * width, (i + 1) * width)
@@ -83,28 +86,55 @@ def tile_regu_diff_kernel(tc, seg, W, out):
 
         def threshold(t):
             wts[t] = wt_pool.tile([P, N], BF16, name="wt")
-            if t == 0:
-                for i in range(2):
-                    threshold_cols(t, slice(i * HALF, (i + 1) * HALF), halves[:, i : i + 1])
-                nc.vector.tensor_tensor(
-                    out=part[:, 0:1], in0=halves[:, 0:1], in1=halves[:, 1:2], op=ALU.add
+            threshold_cols(t, slice(0, N), part[:, t : t + 1])
+
+        folds = {}
+
+        def threshold_by_mask(t):
+            wts[t] = wt_pool.tile([P, N], BF16, name="wt")
+            mask = mask_pool.tile([P, N], BF16, name="mask")
+            pieces = 4 if t == 0 else 2
+            cols = [slice(i * N // pieces, (i + 1) * N // pieces) for i in range(pieces)]
+            for i in range(pieces + 1):
+                if i < pieces:
+                    nc.vector.tensor_scalar(
+                        out=mask[:, cols[i]], in0=wins[t][:, cols[i]], scalar1=THRESH, scalar2=None, op0=ALU.is_gt
+                    )
+                if i >= 1:
+                    done = cols[i - 1]
+                    nc.vector.tensor_tensor(
+                        out=wts[t][:, done], in0=wins[t][:, done], in1=mask[:, done], op=ALU.mult
+                    )
+            folds[t] = psum_t.tile([P, 512], F32, tag="xt", name="fold")
+            for j in range(8):
+                nc.tensor.matmul(
+                    out=folds[t][:],
+                    lhsT=ident_bf[:],
+                    rhs=wts[t][:, 512 * j : 512 * (j + 1)],
+                    start=(j == 0),
+                    stop=(j == 7),
                 )
-            else:
-                threshold_cols(t, slice(0, N), part[:, t : t + 1])
+
+        def sum_fold(t):
+            junk = res_pool.tile([P, 512], F32, name="junk")
+            nc.scalar.activation(out=junk[:], in_=folds[t][:], func=ACT.Copy, accum_out=part[:, t : t + 1])
 
         def reciprocal(t):
             nc.vector.reciprocal(out=recip[:, t : t + 1], in_=part[:, t : t + 1])
 
+        def cut(t):
+            return N - V_COLS if t % 2 == 1 else N
+
         def scale_scalar(t):
             ds[t] = d_pool.tile([P, N], BF16, name="d")
-            if t != LAST:
-                nc.scalar.activation(
-                    out=ds[t][:, :CUT], in_=wts[t][:, :CUT], func=ACT.Copy, scale=recip[:, t : t + 1]
-                )
+            nc.scalar.activation(
+                out=ds[t][:, : cut(t)], in_=wts[t][:, : cut(t)], func=ACT.Copy, scale=recip[:, t : t + 1]
+            )
 
         def scale_vector(t):
-            pieces = [slice(CUT, N)]
-            if t == LAST:
+            pieces = [slice(cut(t), N)] if cut(t) < N else []
+            if t >= LAST - 1:
+                ds[t] = d_pool.tile([P, N], BF16, name="d")
                 pieces = [slice(i * 1024, (i + 1) * 1024) for i in range(BANKS)]
             for cols in pieces:
                 nc.vector.tensor_scalar(
@@ -115,7 +145,7 @@ def tile_regu_diff_kernel(tc, seg, W, out):
             words = rows[:].bitcast(F32)
             banks_of[key] = []
             for bank in range(BANKS):
-                xt = psum_t.tile([P, 2, 2, P], F32, name="xt")
+                xt = psum_t.tile([P, 2, 2, P], F32, tag="xt", name="xt")
                 for gl in range(2):
                     w0 = 256 * (2 * bank + gl)
                     for u in range(2):
@@ -167,37 +197,71 @@ def tile_regu_diff_kernel(tc, seg, W, out):
             nc.sync.dma_start(out=out_flat[:, 512 * q + c0 : 512 * q + c1], in_=res[:, c0:c1])
 
         load(0)
+        load(1)
         nc.sync.dma_start(out=seg_in[:], in_=seg_flat)
-        for t in range(1, AHEAD):
+        for t in range(2, AHEAD):
             load(t)
+        threshold_by_mask(0)
+        sum_fold(0)
+        wts[1] = wt_pool.tile([P, N], BF16, name="wt")
+        threshold_cols(1, slice(0, HALF), halves[:, 0:1])
+        reciprocal(0)
+        scale_scalar(0)
+        threshold_cols(1, slice(HALF, N), halves[:, 1:2])
         turn("seg", seg_in)
         evacuate("seg")
+        scale_vector(0)
+        nc.vector.tensor_tensor(out=part[:, 1:2], in0=halves[:, 0:1], in1=halves[:, 1:2], op=ALU.add)
+        turn(0, ds[0])
 
-        for s in range(TILES + 3):
-            if s + AHEAD < TILES:
-                load(s + AHEAD)
-            if s < TILES:
+        for s in range(1, LAST - 1):
+            if s + AHEAD - 1 < TILES:
+                load(s + AHEAD - 1)
+            if s >= 2:
                 threshold(s)
-            if s == 1:
+            if s == 2:
                 nc.vector.quantize_mx(
                     out=seg_codes[:].bitcast(FP8X4), scales=seg_scales[:], in_=groupeds["seg"][:]
                 )
-            if 0 <= s - 3:
+            if s >= 3:
                 quantise(s - 3)
-            if s < TILES:
-                reciprocal(s)
-                scale_scalar(s)
-            if 0 <= s - 1 < TILES:
+            reciprocal(s)
+            scale_scalar(s)
+            if s >= 2:
                 scale_vector(s - 1)
                 turn(s - 1, ds[s - 1])
-            if 0 <= s - 3:
+            if s >= 3:
                 multiply(s - 3)
-            if 0 <= s - 1 < TILES:
-                evacuate(s - 1)
-            done = s - 3
-            if 0 <= done < TILES - 4 and done % 4 == 3:
-                store(done // 4, 0, 512)
-            if done == TILES - 2:
-                store(done // 4, 0, 384)
-            if done == TILES - 1:
-                store(done // 4, 384, 512)
+            evacuate(s - 1)
+            if s >= 3 and (s - 3) % 4 == 3:
+                store((s - 3) // 4, 0, 512)
+
+        b, c = LAST - 1, LAST
+        threshold_by_mask(b)
+        quantise(b - 3)
+        scale_vector(b - 1)
+        turn(b - 1, ds[b - 1])
+        multiply(b - 3)
+        sum_fold(b)
+        evacuate(b - 1)
+        store(6, 0, 512)
+        threshold_by_mask(c)
+        reciprocal(b)
+        scale_vector(b)
+        turn(b, ds[b])
+        quantise(b - 2)
+        multiply(b - 2)
+        sum_fold(c)
+        evacuate(b)
+        quantise(b - 1)
+        multiply(b - 1)
+        reciprocal(c)
+        scale_vector(c)
+        turn(c, ds[c])
+        evacuate(c)
+        quantise(b)
+        multiply(b)
+        store(7, 0, 384)
+        quantise(c)
+        multiply(c)
+        store(7, 384, 512)

@@ -145,19 +145,20 @@ def tile_regu_diff_kernel(tc, seg, W, out):
             words = rows[:].bitcast(F32)
             banks_of[key] = []
             for bank in range(BANKS):
-                xt = psum_t.tile([P, 2, 2, P], F32, tag="xt", name="xt")
+                xt = psum_t.tile([P, 2, P, 2], F32, tag="xt", name="xt")
                 for gl in range(2):
                     w0 = 256 * (2 * bank + gl)
                     for u in range(2):
-                        nc.tensor.transpose(xt[:, gl, u, :], words[:, w0 + u : w0 + 256 : 2], ident[:])
+                        nc.tensor.transpose(xt[:, gl, :, u], words[:, w0 + u : w0 + 256 : 2], ident[:])
                 banks_of[key].append(xt)
 
         def evacuate(key):
             groupeds[key] = g_pool.tile([P, PASSES * 512], BF16, name="grouped", align_bytes=64)
-            view = groupeds[key][:].bitcast(F32).rearrange("p (b g r u) -> p b g r u", b=BANKS, g=2, u=2)
+            view = groupeds[key][:].bitcast(F32)
             for bank in range(BANKS):
                 nc.scalar.copy(
-                    out=view[:, bank, :, :, :], in_=banks_of[key][bank][:].rearrange("p g u r -> p g r u")
+                    out=view[:, 512 * bank : 512 * (bank + 1)],
+                    in_=banks_of[key][bank][:].rearrange("p g r u -> p (g r u)"),
                 )
 
         def quantise(t):

from contextlib import ExitStack

import concourse.mybir as mybir
from concourse.masks import make_identity

BF16 = mybir.dt.bfloat16
F32 = mybir.dt.float32
U32 = mybir.dt.uint32
U8 = mybir.dt.uint8
FP8X4 = mybir.dt.float8_e4m3fn_x4
ALU = mybir.AluOpType
ACT = mybir.ActivationFunctionType

P = 128
N = 4096
HALF = N // 2
WORDS = N // 2
THRESH = 0.85
TILES = N // P
LAST = TILES - 1
FOLDED = (0, LAST - 1, LAST)
PASSES = N // 512
BANKS = 4
FLOPS = 2 * P * N * N

AHEAD = 4
V_COLS = 1664


def tile_regu_diff_kernel(tc, seg, W, out):
    nc = tc.nc
    seg_flat = seg.rearrange("b d r c -> (b d) (r c)")
    out_flat = out.rearrange("b d r c -> (b d) (r c)")
    w2 = W.rearrange("b m n -> (b m) n")

    with ExitStack() as ctx:
        ctx.enter_context(tc.manual_schedule())
        const = ctx.enter_context(tc.tile_pool(name="const", bufs=1))
        win_pool = ctx.enter_context(tc.tile_pool(name="win", bufs=AHEAD + 2))
        wt_pool = ctx.enter_context(tc.tile_pool(name="wt", bufs=4))
        d_pool = ctx.enter_context(tc.tile_pool(name="d", bufs=4))
        g_pool = ctx.enter_context(tc.tile_pool(name="grouped", bufs=4))
        q_pool = ctx.enter_context(tc.tile_pool(name="quant", bufs=4))
        mask_pool = ctx.enter_context(tc.tile_pool(name="mask", bufs=2))
        res_pool = ctx.enter_context(tc.tile_pool(name="res", bufs=2))
        psum_t = ctx.enter_context(tc.psum_pool(name="psum_t", bufs=6))
        psum_a = ctx.enter_context(tc.psum_pool(name="psum_a", bufs=2))

        ident = const.tile([P, P], F32, name="ident")
        make_identity(nc, ident[:])
        ident_bf = const.tile([P, P], BF16, name="ident_bf")
        make_identity(nc, ident_bf[:])
        part = const.tile([P, TILES], F32, name="part")
        halves = const.tile([P, 2], F32, name="halves")
        recip = const.tile([P, TILES], F32, name="recip")
        seg_in = const.tile([P, N], BF16, name="seg_in")
        seg_codes = const.tile([P, PASSES * P], U32, name="seg_codes", align_bytes=64)
        seg_scales = const.tile([P, PASSES * P], U8, name="seg_scales", align_bytes=64)

        wins = {}
        wts = {}
        ds = {}
        groupeds = {}
        banks_of = {}
        quants = {}
        accs = {}

        def load(t):
            wins[t] = win_pool.tile([P, N], BF16, name="win")
            pieces = {0: 4, 1: 2}.get(t, 1)
            width = N // pieces
            for i in range(pieces):
                cols = slice(i * width, (i + 1) * width)
                nc.sync.dma_start(out=wins[t][:, cols], in_=w2[t * P : (t + 1) * P, cols])

        def threshold_cols(t, cols, total):
            nc.vector.scalar_tensor_tensor(
                out=wts[t][:, cols],
                in0=wins[t][:, cols],
                scalar=THRESH,
                in1=wins[t][:, cols],
                op0=ALU.is_gt,
                op1=ALU.mult,
                accum_out=total,
            )

        def threshold(t):
            wts[t] = wt_pool.tile([P, N], BF16, name="wt")
            threshold_cols(t, slice(0, N), part[:, t : t + 1])

        folds = {}

        def threshold_by_mask(t):
            wts[t] = wt_pool.tile([P, N], BF16, name="wt")
            mask = mask_pool.tile([P, N], BF16, name="mask")
            pieces = 4 if t == 0 else 2
            cols = [slice(i * N // pieces, (i + 1) * N // pieces) for i in range(pieces)]
            for i in range(pieces + 1):
                if i < pieces:
                    nc.vector.tensor_scalar(
                        out=mask[:, cols[i]], in0=wins[t][:, cols[i]], scalar1=THRESH, scalar2=None, op0=ALU.is_gt
                    )
                if i >= 1:
                    done = cols[i - 1]
                    nc.vector.tensor_tensor(
                        out=wts[t][:, done], in0=wins[t][:, done], in1=mask[:, done], op=ALU.mult
                    )
            folds[t] = psum_t.tile([P, 512], F32, tag="xt", name="fold")
            for j in range(8):
                nc.tensor.matmul(
                    out=folds[t][:],
                    lhsT=ident_bf[:],
                    rhs=wts[t][:, 512 * j : 512 * (j + 1)],
                    start=(j == 0),
                    stop=(j == 7),
                )

        def sum_fold(t):
            junk = res_pool.tile([P, 512], F32, name="junk")
            nc.scalar.activation(out=junk[:], in_=folds[t][:], func=ACT.Copy, accum_out=part[:, t : t + 1])

        def reciprocal(t):
            nc.vector.reciprocal(out=recip[:, t : t + 1], in_=part[:, t : t + 1])

        def cut(t):
            return N - V_COLS if t % 2 == 1 else N

        def scale_scalar(t):
            ds[t] = d_pool.tile([P, N], BF16, name="d")
            nc.scalar.activation(
                out=ds[t][:, : cut(t)], in_=wts[t][:, : cut(t)], func=ACT.Copy, scale=recip[:, t : t + 1]
            )

        def scale_vector(t):
            pieces = [slice(cut(t), N)] if cut(t) < N else []
            if t >= LAST - 1:
                ds[t] = d_pool.tile([P, N], BF16, name="d")
                pieces = [slice(i * 1024, (i + 1) * 1024) for i in range(BANKS)]
            for cols in pieces:
                nc.vector.tensor_scalar(
                    out=ds[t][:, cols], in0=wts[t][:, cols], scalar1=recip[:, t : t + 1], scalar2=None, op0=ALU.mult
                )

        def turn(key, rows):
            words = rows[:].bitcast(F32)
            banks_of[key] = []
            for bank in range(BANKS):
                xt = psum_t.tile([P, 2, P, 2], F32, tag="xt", name="xt")
                for gl in range(2):
                    w0 = 256 * (2 * bank + gl)
                    for u in range(2):
                        nc.tensor.transpose(xt[:, gl, :, u], words[:, w0 + u : w0 + 256 : 2], ident[:])
                banks_of[key].append(xt)

        def evacuate(key):
            groupeds[key] = g_pool.tile([P, PASSES * 512], BF16, name="grouped", align_bytes=64)
            view = groupeds[key][:].bitcast(F32)
            for bank in range(BANKS):
                nc.scalar.copy(
                    out=view[:, 512 * bank : 512 * (bank + 1)],
                    in_=banks_of[key][bank][:].rearrange("p g r u -> p (g r u)"),
                )

        def quantise(t):
            codes = q_pool.tile([P, PASSES * P], U32, name="codes", align_bytes=64)
            scales = q_pool.tile([P, PASSES * P], U8, name="scales", align_bytes=64)
            pieces = 4 if t == LAST else 1
            words = PASSES * P // pieces
            for i in range(pieces):
                nc.vector.quantize_mx(
                    out=codes[:, i * words : (i + 1) * words].bitcast(FP8X4),
                    scales=scales[:, i * words : (i + 1) * words],
                    in_=groupeds[t][:, 4 * i * words : 4 * (i + 1) * words],
                )
            quants[t] = (codes, scales)

        def multiply(t):
            if t % 4 == 0:
                accs[t // 4] = psum_a.tile([P, 512], F32, name="acc")
            acc = accs[t // 4]
            codes, scales = quants[t]
            c0 = (t % 4) * P
            for g in range(PASSES):
                cols = slice(g * P, (g + 1) * P)
                nc.tensor.matmul_mx(
                    out=acc[:, c0 : c0 + P],
                    lhsT=seg_codes[:, cols].bitcast(FP8X4),
                    lhsT_scale=seg_scales[:, cols],
                    rhs=codes[:, cols].bitcast(FP8X4),
                    rhs_scale=scales[:, cols],
                    start=(g == 0),
                    stop=(g == PASSES - 1),
                )

        def store(q, c0, c1):
            res = res_pool.tile([P, 512], F32, name="res")
            nc.scalar.copy(out=res[:, c0:c1], in_=accs[q][:, c0:c1])
            nc.sync.dma_start(out=out_flat[:, 512 * q + c0 : 512 * q + c1], in_=res[:, c0:c1])

        load(0)
        load(1)
        nc.sync.dma_start(out=seg_in[:], in_=seg_flat)
        for t in range(2, AHEAD):
            load(t)
        threshold_by_mask(0)
        sum_fold(0)
        wts[1] = wt_pool.tile([P, N], BF16, name="wt")
        threshold_cols(1, slice(0, HALF), halves[:, 0:1])
        reciprocal(0)
        scale_scalar(0)
        threshold_cols(1, slice(HALF, N), halves[:, 1:2])
        turn("seg", seg_in)
        evacuate("seg")
        scale_vector(0)
        nc.vector.tensor_tensor(out=part[:, 1:2], in0=halves[:, 0:1], in1=halves[:, 1:2], op=ALU.add)
        turn(0, ds[0])

        for s in range(1, LAST - 1):
            if s + AHEAD - 1 < TILES:
                load(s + AHEAD - 1)
            if s >= 2:
                threshold(s)
            if s == 2:
                nc.vector.quantize_mx(
                    out=seg_codes[:].bitcast(FP8X4), scales=seg_scales[:], in_=groupeds["seg"][:]
                )
            if s >= 3:
                quantise(s - 3)
            reciprocal(s)
            scale_scalar(s)
            if s >= 2:
                scale_vector(s - 1)
                turn(s - 1, ds[s - 1])
            if s >= 3:
                multiply(s - 3)
            evacuate(s - 1)
            if s >= 3 and (s - 3) % 4 == 3:
                store((s - 3) // 4, 0, 512)

        b, c = LAST - 1, LAST
        threshold_by_mask(b)
        quantise(b - 3)
        scale_vector(b - 1)
        turn(b - 1, ds[b - 1])
        multiply(b - 3)
        sum_fold(b)
        evacuate(b - 1)
        store(6, 0, 512)
        threshold_by_mask(c)
        reciprocal(b)
        scale_vector(b)
        turn(b, ds[b])
        quantise(b - 2)
        multiply(b - 2)
        sum_fold(c)
        evacuate(b)
        quantise(b - 1)
        multiply(b - 1)
        reciprocal(c)
        scale_vector(c)
        turn(c, ds[c])
        evacuate(c)
        quantise(b)
        multiply(b)
        store(7, 0, 384)
        quantise(c)
        multiply(c)
        store(7, 384, 512)
